import numpy as np
import ml_dtypes


def mxq(x, axis, fmt="e4m3"):
    dtype, down = {"e4m3": (ml_dtypes.float8_e4m3fn, 7), "e5m2": (ml_dtypes.float8_e5m2, 14)}[fmt]
    v = np.moveaxis(np.asarray(x, np.float32).astype(ml_dtypes.bfloat16).astype(np.float64), axis, -1)
    blocks = v.reshape(v.shape[:-1] + (-1, 32))
    amax = np.abs(blocks).max(-1, keepdims=True)
    byte = np.maximum(np.where(amax > 0, np.frexp(amax)[1] - 1 + 127, 0) - down, 1)
    scale = np.exp2(byte - 127.0)
    codes = (blocks / scale).astype(np.float32).astype(dtype).astype(np.float64)
    return np.moveaxis((codes * scale).reshape(v.shape), -1, axis)


WIDE = False


def mx_kscale(k):
    if not WIDE:
        return np.ones(k)
    levels = np.array([10, -10, 5, -5, 0])
    if k % 512:
        return np.exp2(np.random.permutation(np.resize(levels, k // 32))).repeat(32)
    a = np.empty((k // 512, 16))
    for p in range(k // 512):
        a[p, :8] = np.random.permutation(np.resize(levels, 8))
        for g in range(8):
            far = levels[np.abs(levels - a[p, g]) >= 10]
            a[p, g + 8] = far[np.random.randint(len(far))]
    return np.exp2(a.ravel()).repeat(32)


BF16 = ml_dtypes.bfloat16


def bf(x):
    return np.asarray(x, np.float32).astype(BF16)


def f64(x):
    return np.asarray(x).astype(np.float64)


NA, NB, ND, ED = 64, 64, 1024, 512
K1 = 2 * ED


def draw0():
    s, t = mx_kscale(K1), mx_kscale(ED)
    return {"edge_embeds": bf(np.random.standard_normal((NA, NB, K1)) * s),
            "a_proj": bf(np.random.standard_normal((NA, ED)) * 0.5 * t),
            "b_proj": bf(np.random.standard_normal((NB, ED)) * 0.5 * t),
            "We": bf(np.random.standard_normal((K1, ED)) * 0.7 / np.sqrt(K1) / s[:, None] * t),
            "be1": bf(np.random.standard_normal(ED) * 0.3 * t),
            "We2": bf(np.random.standard_normal((ED, ED)) * 0.5 / np.sqrt(ED) / t[:, None]),
            "be2": bf(np.random.standard_normal(ED) * 0.1)}


def core(edge_embeds, a_proj, b_proj, We, be1, We2, be2):
    h = f64(a_proj)[:, None, :] + f64(b_proj)[None, :, :] + (mxq(f64(edge_embeds), 2, "e4m3") @ mxq(f64(We), 0, "e4m3")) + f64(be1)
    h = np.maximum(h, 0.0)
    edge_latent = np.maximum((mxq(h, 2, "e4m3") @ mxq(f64(We2), 0, "e4m3")) + f64(be2), 0.0)
    sum_a = edge_latent.sum(axis=1)
    sum_b = edge_latent.sum(axis=0)
    return edge_latent, sum_a, sum_b


def e4m3fn_bytes(y):
    return np.clip(np.asarray(y, np.float64), -448.0, 448.0).astype(np.float32).astype(ml_dtypes.float8_e4m3fn).view(np.uint8)


def e4m3fn_values(b):
    return np.asarray(b, np.uint8).view(ml_dtypes.float8_e4m3fn).astype(np.float64)


def setup_inputs():
    d = draw0()
    x0 = np.asarray(d['edge_embeds']).astype(np.float64)
    s = (np.max(np.abs(x0), axis=(0, 1), keepdims=True) / 448.0).astype(np.float32)
    out = {}
    for k, v in d.items():
        if k == 'edge_embeds':
            out['edge_embeds_bytes'] = e4m3fn_bytes(x0 / s.astype(np.float64))
            out['edge_embeds_scale'] = s
        else:
            out[k] = v
    return out


def reference(edge_embeds_bytes, edge_embeds_scale, a_proj, b_proj, We, be1, We2, be2):
    return core(e4m3fn_values(edge_embeds_bytes) * edge_embeds_scale.astype(np.float64), a_proj, b_proj, We, be1, We2, be2)

@@ -1,0 +1,303 @@
+from contextlib import ExitStack
+
+import concourse.mybir as mybir
+from concourse.masks import make_identity
+
+NA, NB, K1, ED = 64, 64, 1024, 512
+E = NA * NB
+FLOPS = 2 * E * (K1 * ED + ED * ED)
+
+F32 = mybir.dt.float32
+BF16 = mybir.dt.bfloat16
+U32 = mybir.dt.uint32
+U8 = mybir.dt.uint8
+FP8 = mybir.dt.float8_e4m3fn
+FP8X4 = mybir.dt.float8_e4m3fn_x4
+ADD = mybir.AluOpType.add
+MULT = mybir.AluOpType.mult
+AXIS_X = mybir.AxisListType.X
+RELU = mybir.ActivationFunctionType.Relu
+
+P = 128
+TILES = E // P
+GROUP = 4
+WIN = 2 * GROUP + NB
+
+
+def tile_bipartiteneuralmessagepassinglayer_pa_t_kernel(
+    tc, x_bytes, x_scale, a_proj, b_proj, we, be1, we2, be2, out_edge, out_a, out_b
+):
+    nc = tc.nc
+    x_rows = x_bytes.rearrange("i j k -> (i j) k")
+    out_rows = out_edge.rearrange("i j c -> (i j) c")
+
+    with ExitStack() as ctx:
+        keep = ctx.enter_context(tc.tile_pool(name="keep", bufs=1))
+        work = ctx.enter_context(tc.tile_pool(name="work", bufs=3))
+        psum = ctx.enter_context(tc.psum_pool(name="psum", bufs=1))
+        ctx.enter_context(tc.manual_schedule())
+
+        byte_tiles, wide, turned, grouped, x_codes = {}, {}, {}, {}, {}
+        addend, hidden, h_codes, acc1, acc2, lat = {}, {}, {}, {}, {}, {}
+
+        def load(n):
+            tile_bytes = work.tile([P, K1], U8, tag="bytes", bufs=7, name="tile_bytes")
+            nc.sync.dma_start(out=tile_bytes[:], in_=x_rows[n * P : (n + 1) * P, :])
+            byte_tiles[n] = tile_bytes
+
+        load(0)
+        scale = keep.tile([P, 2, 4], F32, name="scale")
+        nc.scalar.dma_start(out=scale[:], in_=x_scale.rearrange("a b (g p t) -> p (a b g) t", p=P, t=4))
+        we_raw = []
+        for g in range(2):
+            raw = keep.tile([P, 4, ED], BF16, name="we_raw%d" % g)
+            nc.sync.dma_start(out=raw[:], in_=we[g * 512 : (g + 1) * 512, :].rearrange("(p j) c -> p j c", j=4))
+            we_raw.append(raw)
+            load(1 + g)
+        ab = keep.tile([P, ED], BF16, name="ab")
+        nc.scalar.dma_start(out=ab[0:NA, :], in_=a_proj)
+        nc.scalar.dma_start(out=ab[NA:P, :], in_=b_proj)
+        be1_col = keep.tile([P, 4], BF16, name="be1_col")
+        nc.scalar.dma_start(out=be1_col[:], in_=be1.rearrange("(p t) -> p t", t=4))
+        load(3)
+        w2_raw = keep.tile([P, 4, ED], BF16, name="w2_raw")
+        nc.sync.dma_start(out=w2_raw[:], in_=we2.rearrange("(p j) c -> p j c", j=4))
+        be2_all = keep.tile([P, ED], BF16, name="be2_all")
+        nc.sync.dma_start(out=be2_all[:], in_=be2.partition_broadcast(P))
+        load(4)
+        load(5)
+
+        ident = keep.tile([P, P], F32, name="ident")
+        make_identity(nc, ident[:])
+        ident_bf = keep.tile([P, P], BF16, name="ident_bf")
+        nc.vector.tensor_copy(out=ident_bf[:], in_=ident[:])
+        sel = keep.tile([P, GROUP, WIN], F32, name="sel")
+        nc.vector.memset(sel[:], 0.0)
+        for q in range(GROUP):
+            nc.vector.tensor_reduce(
+                out=sel[:, q, 2 * q : 2 * q + 2], in_=ident[:].rearrange("p (h j) -> p h j", h=2), axis=AXIS_X, op=ADD
+            )
+            nc.vector.tensor_reduce(
+                out=sel[:, q, 2 * GROUP :], in_=ident[:].rearrange("p (h j) -> p j h", h=2), axis=AXIS_X, op=ADD
+            )
+        sums = keep.tile([P, 4, P], F32, name="sums")
+
+        we_codes = keep.tile([P, 2, ED], U32, align_bytes=64, name="we_codes")
+        we_planes = keep.tile([P, 2, ED], U8, align_bytes=64, name="we_planes")
+        w2_codes = keep.tile([P, ED], U32, align_bytes=64, name="w2_codes")
+        w2_planes = keep.tile([P, ED], U8, align_bytes=64, name="w2_planes")
+        we_grouped = [keep.tile([P, 4, P, 4], BF16, align_bytes=64, name="we_grouped%d" % g) for g in range(2)]
+        w2_grouped = keep.tile([P, ED, 4], BF16, align_bytes=64, name="w2_grouped")
+
+        def we_view(g, lo, hi):
+            return we_raw[g][:].rearrange("p j (m t) -> p t m j", t=4)[:, lo:hi]
+
+        def we_quantize(g):
+            nc.vector.quantize_mx(
+                out=we_codes[:, g, :].bitcast(FP8X4),
+                scales=we_planes[:, g, :],
+                in_=we_grouped[g][:].rearrange("p t m j -> p (t m j)"),
+            )
+
+        def widen(n):
+            wide[n] = work.tile([P, K1], BF16, tag="wide", name="wide_tile")
+            nc.scalar.copy(out=wide[n][:], in_=byte_tiles[n][:].bitcast(FP8))
+
+        def turn(n):
+            turned[n] = psum.tile([P, 2, P, 2], F32, tag="xt", bufs=3, name="turned_tile")
+            words = wide[n][:].bitcast(F32)
+            for g in range(2):
+                for u in range(2):
+                    nc.tensor.transpose(
+                        turned[n][:, g, :, u], words[:, 256 * g + u : 256 * (g + 1) : 2], ident[:]
+                    )
+
+        def product(n):
+            grouped[n] = work.tile([P, 2, 512], BF16, tag="xg", align_bytes=64, name="grouped_tile")
+            values = turned[n][:].rearrange("p g r u -> p (g r u)").bitcast(BF16)
+            nc.vector.tensor_tensor(
+                out=grouped[n][:].rearrange("p g (r t) -> p g r t", t=4),
+                in0=values.rearrange("p (g r t) -> p g r t", g=2, t=4),
+                in1=scale[:].unsqueeze(2).to_broadcast([P, 2, P, 4]),
+                op=MULT,
+            )
+
+        def quantize_x(n):
+            codes = work.tile([P, 2, P], U32, tag="xq", align_bytes=64, name="x_code_tile")
+            planes = work.tile([P, 2, P], U8, tag="xs", align_bytes=64, name="x_plane_tile")
+            nc.vector.quantize_mx(
+                out=codes[:].rearrange("p g r -> p (g r)").bitcast(FP8X4),
+                scales=planes[:].rearrange("p g r -> p (g r)"),
+                in_=grouped[n][:].rearrange("p g w -> p (g w)"),
+            )
+            x_codes[n] = (codes, planes)
+
+        def first_matmul(n):
+            acc1[n] = psum.tile([P, 4, P], F32, tag="s1", bufs=2, name="acc1_tile")
+            codes, planes = x_codes[n]
+            for t in range(4):
+                for g in range(2):
+                    nc.tensor.matmul_mx(
+                        out=acc1[n][:, t, :],
+                        lhsT=we_codes[:, g, t * P : (t + 1) * P].bitcast(FP8X4),
+                        lhsT_scale=we_planes[:, g, t * P : (t + 1) * P],
+                        rhs=codes[:, g, :].bitcast(FP8X4),
+                        rhs_scale=planes[:, g, :],
+                        start=(g == 0),
+                        stop=(g == 1),
+                    )
+
+        def make_addend(n):
+            addend[n] = work.tile([P, 2, NB, 4], F32, tag="addend", bufs=1, name="addend_tile")
+            for i in range(2):
+                nc.gpsimd.tensor_tensor(
+                    out=addend[n][:, i],
+                    in0=b_cols[:],
+                    in1=a_cols[:, 2 * n + i, :].unsqueeze(1).to_broadcast([P, NB, 4]),
+                    op=ADD,
+                )
+
+        def add_terms(n):
+            hidden[n] = work.tile([P, P, 4], BF16, tag="hid", align_bytes=64, name="hidden_tile")
+            nc.vector.tensor_tensor(
+                out=hidden[n][:],
+                in0=acc1[n][:].rearrange("p t e -> p e t"),
+                in1=addend[n][:].rearrange("p i j t -> p (i j) t"),
+                op=ADD,
+            )
+
+        def relu_hidden(n):
+            positive = work.tile([P, P * 4], BF16, tag="pos", align_bytes=64, name="positive_tile")
+            nc.scalar.activation(out=positive[:], in_=hidden[n][:].rearrange("p e t -> p (e t)"), func=RELU)
+            hidden[n] = positive
+
+        def quantize_h(n):
+            codes = work.tile([P, P], U32, tag="hq", align_bytes=64, name="h_code_tile")
+            planes = work.tile([P, P], U8, tag="hs", align_bytes=64, name="h_plane_tile")
+            nc.vector.quantize_mx(out=codes[:].bitcast(FP8X4), scales=planes[:], in_=hidden[n][:])
+            h_codes[n] = (codes, planes)
+
+        def second_matmul(n):
+            acc2[n] = psum.tile([P, ED], F32, tag="s2", bufs=2, name="acc2_tile")
+            codes, planes = h_codes[n]
+            nc.tensor.matmul_mx(
+                out=acc2[n][:],
+                lhsT=codes[:].bitcast(FP8X4),
+                lhsT_scale=planes[:],
+                rhs=w2_codes[:].bitcast(FP8X4),
+                rhs_scale=w2_planes[:],
+                start=True,
+                stop=True,
+            )
+
+        def add_bias(n):
+            lat[n] = work.tile([P, ED], F32, tag="lat", bufs=11, name="lat_tile")
+            nc.vector.tensor_tensor(out=lat[n][:], in0=acc2[n][:], in1=be2_all[:], op=ADD)
+
+        def finish(n):
+            nc.scalar.activation(out=lat[n][:], in_=lat[n][:], func=RELU)
+            nc.sync.dma_start(out=out_rows[n * P : (n + 1) * P, :], in_=lat[n][:])
+
+        sum_banks = {}
+
+        def sum_block(group, cb):
+            if cb == 0:
+                sum_banks[group] = psum.tile([P, 4, WIN], F32, tag="sum", bufs=1, name="sum_tile")
+            for q in range(GROUP):
+                nc.tensor.matmul(
+                    out=sum_banks[group][:, cb, :],
+                    lhsT=lat[group * GROUP + q][:, cb * P : (cb + 1) * P],
+                    rhs=sel[:, q, :],
+                    start=(q == 0),
+                    stop=(q == GROUP - 1),
+                )
+
+        def sum_out(group):
+            bank = sum_banks[group]
+            first = 2 * GROUP * group
+            nc.scalar.copy(out=sums[:, :, first : first + 2 * GROUP], in_=bank[:, :, 0 : 2 * GROUP])
+            if group == 0:
+                nc.scalar.copy(out=sums[:, :, NA:P], in_=bank[:, :, 2 * GROUP :])
+            else:
+                part = work.tile([P, 4, NB], F32, tag="part", name="part_tile")
+                nc.scalar.copy(out=part[:], in_=bank[:, :, 2 * GROUP :])
+                nc.gpsimd.tensor_tensor(out=sums[:, :, NA:P], in0=sums[:, :, NA:P], in1=part[:], op=ADD)
+
+        ab_turned = psum.tile([P, 4, P], BF16, tag="xt", bufs=3, name="ab_turned")
+        widen(0)
+        nc.vector.tensor_copy(out=we_grouped[0][:, 0:2], in_=we_view(0, 0, 2))
+        nc.scalar.copy(out=we_grouped[0][:, 2:4], in_=we_view(0, 2, 4))
+        turn(0)
+        for t in range(4):
+            nc.tensor.transpose(ab_turned[:, t, :], ab[:, t:ED:4], ident_bf[:])
+        nc.scalar.copy(out=we_grouped[1][:, 2:4], in_=we_view(1, 2, 4))
+        product(0)
+        nc.vector.tensor_copy(out=we_grouped[1][:, 0:2], in_=we_view(1, 0, 2))
+        we_quantize(0)
+        quantize_x(0)
+        we_quantize(1)
+        a_cols = keep.tile([P, NA, 4], F32, name="a_cols")
+        b_cols = keep.tile([P, NB, 4], F32, name="b_cols")
+        nc.vector.tensor_tensor(
+            out=a_cols[:],
+            in0=ab_turned[:, :, 0:NA].rearrange("p t n -> p n t"),
+            in1=be1_col[:].unsqueeze(1).to_broadcast([P, NA, 4]),
+            op=ADD,
+        )
+        nc.vector.tensor_copy(out=b_cols[:], in_=ab_turned[:, :, NA:P].rearrange("p t n -> p n t"))
+        make_addend(0)
+        widen(1)
+        turn(1)
+
+        for n in range(1, TILES + 2 + 5):
+            def live(m):
+                return 0 <= m < TILES
+
+            if live(n - 1):
+                first_matmul(n - 1)
+            if live(n - 2):
+                second_matmul(n - 2)
+            done = n - 6
+            if done >= 0 and done // GROUP < TILES // GROUP:
+                sum_block(done // GROUP, done % GROUP)
+            if live(n + 5):
+                load(n + 5)
+            if live(n + 1):
+                widen(n + 1)
+                turn(n + 1)
+            if live(n):
+                product(n)
+            if live(n - 1):
+                add_terms(n - 1)
+                relu_hidden(n - 1)
+            if live(n):
+                make_addend(n)
+            if live(n - 2):
+                add_bias(n - 2)
+                finish(n - 2)
+            if live(n):
+                quantize_x(n)
+            if live(n - 1):
+                quantize_h(n - 1)
+            if n == 1:
+                nc.scalar.copy(
+                    out=w2_grouped[:, 0 : ED // 2], in_=w2_raw[:, :, 0 : ED // 2].rearrange("p j c -> p c j")
+                )
+                nc.vector.tensor_copy(
+                    out=w2_grouped[:, ED // 2 :], in_=w2_raw[:, :, ED // 2 :].rearrange("p j c -> p c j")
+                )
+                nc.vector.quantize_mx(
+                    out=w2_codes[:].bitcast(FP8X4),
+                    scales=w2_planes[:],
+                    in_=w2_grouped[:].rearrange("p c j -> p (c j)"),
+                )
+            if done >= 0 and done % GROUP == GROUP - 1 and done // GROUP < TILES // GROUP:
+                sum_out(done // GROUP)
+
+        sums_turned = psum.tile([P, 4, P], F32, tag="xt", bufs=3, name="sums_turned")
+        for cb in range(4):
+            nc.tensor.transpose(sums_turned[:, cb, :], sums[:, cb, :], ident[:])
+        result = keep.tile([P, ED], F32, name="result")
+        nc.vector.tensor_copy(out=result[:], in_=sums_turned[:].rearrange("p c m -> p (c m)"))
+        nc.sync.dma_start(out=out_a, in_=result[0:NA, :])
+        nc.sync.dma_start(out=out_b, in_=result[NA:P, :])

@@ -20,8 +20,7 @@ RELU = mybir.ActivationFunctionType.Relu
 
 P = 128
 TILES = E // P
-GROUP = 4
-WIN = 2 * GROUP + NB
+SEL_STEP = P + 2
 
 
 def tile_bipartiteneuralmessagepassinglayer_pa_t_kernel(
@@ -71,16 +70,21 @@ def tile_bipartiteneuralmessagepassinglayer_pa_t_kernel(
         make_identity(nc, ident[:])
         ident_bf = keep.tile([P, P], BF16, name="ident_bf")
         nc.vector.tensor_copy(out=ident_bf[:], in_=ident[:])
-        sel = keep.tile([P, GROUP, WIN], F32, name="sel")
-        nc.vector.memset(sel[:], 0.0)
-        for q in range(GROUP):
-            nc.vector.tensor_reduce(
-                out=sel[:, q, 2 * q : 2 * q + 2], in_=ident[:].rearrange("p (h j) -> p h j", h=2), axis=AXIS_X, op=ADD
-            )
-            nc.vector.tensor_reduce(
-                out=sel[:, q, 2 * GROUP :], in_=ident[:].rearrange("p (h j) -> p j h", h=2), axis=AXIS_X, op=ADD
-            )
-        sums = keep.tile([P, 4, P], F32, name="sums")
+        sel = keep.tile([P, NB + TILES * SEL_STEP], F32, name="sel")
+        nc.gpsimd.memset(sel[:], 0.0)
+        halves = keep.tile([P, 2], F32, name="halves")
+        nc.vector.tensor_reduce(out=halves[:], in_=ident[:].rearrange("p (h j) -> p h j", h=2), axis=AXIS_X, op=ADD)
+        inner = keep.tile([P, NB], F32, name="inner")
+        nc.vector.tensor_reduce(out=inner[:], in_=ident[:].rearrange("p (h j) -> p j h", h=2), axis=AXIS_X, op=ADD)
+        nc.vector.tensor_copy(
+            out=sel[:, 0 : TILES * P].rearrange("p (n m) -> p n m", m=P)[:, :, 0:NB],
+            in_=inner[:].unsqueeze(1).to_broadcast([P, TILES, NB]),
+        )
+        nc.vector.tensor_copy(
+            out=sel[:, NB:].rearrange("p (n m) -> p n m", m=SEL_STEP)[:, :, 0:2],
+            in_=halves[:].unsqueeze(1).to_broadcast([P, TILES, 2]),
+        )
+        sums = psum.tile([P, ED], F32, tag="sum", bufs=1, name="sums")
 
         we_codes = keep.tile([P, 2, ED], U32, align_bytes=64, name="we_codes")
         we_planes = keep.tile([P, 2, ED], U8, align_bytes=64, name="we_planes")
@@ -191,51 +195,31 @@ def tile_bipartiteneuralmessagepassinglayer_pa_t_kernel(
             )
 
         def add_bias(n):
-            lat[n] = work.tile([P, ED], F32, tag="lat", bufs=11, name="lat_tile")
+            lat[n] = work.tile([P, ED], F32, tag="lat", bufs=6, name="lat_tile")
             nc.vector.tensor_tensor(out=lat[n][:], in0=acc2[n][:], in1=be2_all[:], op=ADD)
 
         def finish(n):
             nc.scalar.activation(out=lat[n][:], in_=lat[n][:], func=RELU)
             nc.sync.dma_start(out=out_rows[n * P : (n + 1) * P, :], in_=lat[n][:])
 
-        sum_banks = {}
-
-        def sum_block(group, cb):
-            if cb == 0:
-                sum_banks[group] = psum.tile([P, 4, WIN], F32, tag="sum", bufs=1, name="sum_tile")
-            for q in range(GROUP):
-                nc.tensor.matmul(
-                    out=sum_banks[group][:, cb, :],
-                    lhsT=lat[group * GROUP + q][:, cb * P : (cb + 1) * P],
-                    rhs=sel[:, q, :],
-                    start=(q == 0),
-                    stop=(q == GROUP - 1),
-                )
-
-        def sum_out(group):
-            bank = sum_banks[group]
-            first = 2 * GROUP * group
-            nc.scalar.copy(out=sums[:, :, first : first + 2 * GROUP], in_=bank[:, :, 0 : 2 * GROUP])
-            if group == 0:
-                nc.scalar.copy(out=sums[:, :, NA:P], in_=bank[:, :, 2 * GROUP :])
-            else:
-                part = work.tile([P, 4, NB], F32, tag="part", name="part_tile")
-                nc.scalar.copy(out=part[:], in_=bank[:, :, 2 * GROUP :])
-                nc.gpsimd.tensor_tensor(out=sums[:, :, NA:P], in0=sums[:, :, NA:P], in1=part[:], op=ADD)
+        def sum_tile(n):
+            nc.tensor.matmul(
+                out=sums[:],
+                lhsT=sel[:, n * P : (n + 1) * P],
+                rhs=lat[n][:],
+                start=(n == 0),
+                stop=(n == TILES - 1),
+            )
 
         ab_turned = psum.tile([P, 4, P], BF16, tag="xt", bufs=3, name="ab_turned")
         widen(0)
         nc.vector.tensor_copy(out=we_grouped[0][:, 0:2], in_=we_view(0, 0, 2))
-        nc.scalar.copy(out=we_grouped[0][:, 2:4], in_=we_view(0, 2, 4))
         turn(0)
         for t in range(4):
             nc.tensor.transpose(ab_turned[:, t, :], ab[:, t:ED:4], ident_bf[:])
+        nc.scalar.copy(out=we_grouped[0][:, 2:4], in_=we_view(0, 2, 4))
+        widen(1)
         nc.scalar.copy(out=we_grouped[1][:, 2:4], in_=we_view(1, 2, 4))
-        product(0)
-        nc.vector.tensor_copy(out=we_grouped[1][:, 0:2], in_=we_view(1, 0, 2))
-        we_quantize(0)
-        quantize_x(0)
-        we_quantize(1)
         a_cols = keep.tile([P, NA, 4], F32, name="a_cols")
         b_cols = keep.tile([P, NB, 4], F32, name="b_cols")
         nc.vector.tensor_tensor(
@@ -245,40 +229,42 @@ def tile_bipartiteneuralmessagepassinglayer_pa_t_kernel(
             op=ADD,
         )
         nc.vector.tensor_copy(out=b_cols[:], in_=ab_turned[:, :, NA:P].rearrange("p t n -> p n t"))
-        make_addend(0)
-        widen(1)
         turn(1)
 
-        for n in range(1, TILES + 2 + 5):
+        for n in range(TILES + 4):
             def live(m):
                 return 0 <= m < TILES
 
             if live(n - 1):
                 first_matmul(n - 1)
+            if live(n - 3):
+                second_matmul(n - 3)
+            if live(n - 4):
+                sum_tile(n - 4)
+            if live(n + 6):
+                load(n + 6)
             if live(n - 2):
-                second_matmul(n - 2)
-            done = n - 6
-            if done >= 0 and done // GROUP < TILES // GROUP:
-                sum_block(done // GROUP, done % GROUP)
-            if live(n + 5):
-                load(n + 5)
-            if live(n + 1):
-                widen(n + 1)
-                turn(n + 1)
+                add_terms(n - 2)
+                relu_hidden(n - 2)
+            if live(n - 1):
+                make_addend(n - 1)
+            if live(n + 2):
+                widen(n + 2)
+                turn(n + 2)
             if live(n):
                 product(n)
-            if live(n - 1):
-                add_terms(n - 1)
-                relu_hidden(n - 1)
-            if live(n):
-                make_addend(n)
-            if live(n - 2):
-                add_bias(n - 2)
-                finish(n - 2)
+            if n == 0:
+                nc.vector.tensor_copy(out=we_grouped[1][:, 0:2], in_=we_view(1, 0, 2))
+                we_quantize(0)
+            if live(n - 3):
+                add_bias(n - 3)
+                finish(n - 3)
             if live(n):
                 quantize_x(n)
-            if live(n - 1):
-                quantize_h(n - 1)
+            if n == 0:
+                we_quantize(1)
+            if live(n - 2):
+                quantize_h(n - 2)
             if n == 1:
                 nc.scalar.copy(
                     out=w2_grouped[:, 0 : ED // 2], in_=w2_raw[:, :, 0 : ED // 2].rearrange("p j c -> p c j")
@@ -291,13 +277,8 @@ def tile_bipartiteneuralmessagepassinglayer_pa_t_kernel(
                     scales=w2_planes[:],
                     in_=w2_grouped[:].rearrange("p c j -> p (c j)"),
                 )
-            if done >= 0 and done % GROUP == GROUP - 1 and done // GROUP < TILES // GROUP:
-                sum_out(done // GROUP)
 
-        sums_turned = psum.tile([P, 4, P], F32, tag="xt", bufs=3, name="sums_turned")
-        for cb in range(4):
-            nc.tensor.transpose(sums_turned[:, cb, :], sums[:, cb, :], ident[:])
         result = keep.tile([P, ED], F32, name="result")
-        nc.vector.tensor_copy(out=result[:], in_=sums_turned[:].rearrange("p c m -> p (c m)"))
-        nc.sync.dma_start(out=out_a, in_=result[0:NA, :])
-        nc.sync.dma_start(out=out_b, in_=result[NA:P, :])
+        nc.vector.tensor_copy(out=result[:], in_=sums[:])
+        nc.sync.dma_start(out=out_b, in_=result[0:NB, :])
+        nc.sync.dma_start(out=out_a, in_=result[NB:P, :])

@@ -16,6 +16,7 @@ FP8X4 = mybir.dt.float8_e4m3fn_x4
 ADD = mybir.AluOpType.add
 MULT = mybir.AluOpType.mult
 AXIS_X = mybir.AxisListType.X
+COPY = mybir.ActivationFunctionType.Copy
 RELU = mybir.ActivationFunctionType.Relu
 
 P = 128
@@ -47,17 +48,17 @@ def tile_bipartiteneuralmessagepassinglayer_pa_t_kernel(
         load(0)
         scale = keep.tile([P, 2, 4], F32, name="scale")
         nc.scalar.dma_start(out=scale[:], in_=x_scale.rearrange("a b (g p t) -> p (a b g) t", p=P, t=4))
+        ab = keep.tile([P, ED], BF16, name="ab")
+        nc.scalar.dma_start(out=ab[0:NA, :], in_=a_proj)
+        nc.scalar.dma_start(out=ab[NA:P, :], in_=b_proj)
+        be1_col = keep.tile([P, 4], BF16, name="be1_col")
+        nc.scalar.dma_start(out=be1_col[:], in_=be1.rearrange("(p t) -> p t", t=4))
         we_raw = []
         for g in range(2):
             raw = keep.tile([P, 4, ED], BF16, name="we_raw%d" % g)
             nc.sync.dma_start(out=raw[:], in_=we[g * 512 : (g + 1) * 512, :].rearrange("(p j) c -> p j c", j=4))
             we_raw.append(raw)
             load(1 + g)
-        ab = keep.tile([P, ED], BF16, name="ab")
-        nc.scalar.dma_start(out=ab[0:NA, :], in_=a_proj)
-        nc.scalar.dma_start(out=ab[NA:P, :], in_=b_proj)
-        be1_col = keep.tile([P, 4], BF16, name="be1_col")
-        nc.scalar.dma_start(out=be1_col[:], in_=be1.rearrange("(p t) -> p t", t=4))
         load(3)
         w2_raw = keep.tile([P, 4, ED], BF16, name="w2_raw")
         nc.sync.dma_start(out=w2_raw[:], in_=we2.rearrange("(p j) c -> p j c", j=4))
@@ -71,20 +72,21 @@ def tile_bipartiteneuralmessagepassinglayer_pa_t_kernel(
         ident_bf = keep.tile([P, P], BF16, name="ident_bf")
         nc.vector.tensor_copy(out=ident_bf[:], in_=ident[:])
         sel = keep.tile([P, NB + TILES * SEL_STEP], F32, name="sel")
-        nc.gpsimd.memset(sel[:], 0.0)
         halves = keep.tile([P, 2], F32, name="halves")
         nc.vector.tensor_reduce(out=halves[:], in_=ident[:].rearrange("p (h j) -> p h j", h=2), axis=AXIS_X, op=ADD)
         inner = keep.tile([P, NB], F32, name="inner")
         nc.vector.tensor_reduce(out=inner[:], in_=ident[:].rearrange("p (h j) -> p j h", h=2), axis=AXIS_X, op=ADD)
-        nc.vector.tensor_copy(
-            out=sel[:, 0 : TILES * P].rearrange("p (n m) -> p n m", m=P)[:, :, 0:NB],
-            in_=inner[:].unsqueeze(1).to_broadcast([P, TILES, NB]),
-        )
-        nc.vector.tensor_copy(
-            out=sel[:, NB:].rearrange("p (n m) -> p n m", m=SEL_STEP)[:, :, 0:2],
-            in_=halves[:].unsqueeze(1).to_broadcast([P, TILES, 2]),
-        )
         sums = psum.tile([P, ED], F32, tag="sum", bufs=1, name="sums")
+
+        def make_selectors(lo, hi):
+            by_tile = sel[:, lo * P : hi * P].rearrange("p (n m) -> p n m", m=P)
+            wide_inner = inner[:].unsqueeze(1).to_broadcast([P, hi - lo, NB])
+            nc.scalar.copy(out=by_tile[:, :, 0:NB], in_=wide_inner)
+            nc.scalar.activation(out=by_tile[:, :, NB:P], in_=wide_inner, func=COPY, scale=0.0)
+            nc.scalar.copy(
+                out=sel[:, NB + lo * SEL_STEP : NB + hi * SEL_STEP].rearrange("p (n m) -> p n m", m=SEL_STEP)[:, :, 0:2],
+                in_=halves[:].unsqueeze(1).to_broadcast([P, hi - lo, 2]),
+            )
 
         we_codes = keep.tile([P, 2, ED], U32, align_bytes=64, name="we_codes")
         we_planes = keep.tile([P, 2, ED], U8, align_bytes=64, name="we_planes")
@@ -96,6 +98,25 @@ def tile_bipartiteneuralmessagepassinglayer_pa_t_kernel(
         def we_view(g, lo, hi):
             return we_raw[g][:].rearrange("p j (m t) -> p t m j", t=4)[:, lo:hi]
 
+        def regroup(engine, out, in_):
+            if engine == "g":
+                nc.gpsimd.tensor_scalar(out=out, in0=in_, scalar1=1.0, scalar2=0.0, op0=MULT, op1=ADD)
+            elif engine == "s":
+                nc.scalar.copy(out=out, in_=in_)
+            else:
+                nc.vector.tensor_copy(out=out, in_=in_)
+
+        def we_group(engine, g, lo, hi):
+            regroup(engine, we_grouped[g][:, lo:hi], we_view(g, lo, hi))
+
+        def w2_group(engine, lo, hi):
+            regroup(engine, w2_grouped[:, lo:hi], w2_raw[:, :, lo:hi].rearrange("p j c -> p c j"))
+
+        def w2_quantize():
+            nc.vector.quantize_mx(
+                out=w2_codes[:].bitcast(FP8X4), scales=w2_planes[:], in_=w2_grouped[:].rearrange("p c j -> p (c j)")
+            )
+
         def we_quantize(g):
             nc.vector.quantize_mx(
                 out=we_codes[:, g, :].bitcast(FP8X4),
@@ -103,12 +124,15 @@ def tile_bipartiteneuralmessagepassinglayer_pa_t_kernel(
                 in_=we_grouped[g][:].rearrange("p t m j -> p (t m j)"),
             )
 
-        def widen(n):
-            wide[n] = work.tile([P, K1], BF16, tag="wide", name="wide_tile")
-            nc.scalar.copy(out=wide[n][:], in_=byte_tiles[n][:].bitcast(FP8))
+        def widen(n, vector=False):
+            wide[n] = work.tile([P, K1], BF16, tag="wide", bufs=5, name="wide_tile")
+            if vector:
+                nc.vector.tensor_copy(out=wide[n][:], in_=byte_tiles[n][:].bitcast(FP8))
+            else:
+                nc.scalar.copy(out=wide[n][:], in_=byte_tiles[n][:].bitcast(FP8))
 
         def turn(n):
-            turned[n] = psum.tile([P, 2, P, 2], F32, tag="xt", bufs=3, name="turned_tile")
+            turned[n] = psum.tile([P, 2, P, 2], F32, tag="xt", bufs=4, name="turned_tile")
             words = wide[n][:].bitcast(F32)
             for g in range(2):
                 for u in range(2):
@@ -152,7 +176,7 @@ def tile_bipartiteneuralmessagepassinglayer_pa_t_kernel(
                     )
 
         def make_addend(n):
-            addend[n] = work.tile([P, 2, NB, 4], F32, tag="addend", bufs=1, name="addend_tile")
+            addend[n] = work.tile([P, 2, NB, 4], F32, tag="addend", bufs=2, name="addend_tile")
             for i in range(2):
                 nc.gpsimd.tensor_tensor(
                     out=addend[n][:, i],
@@ -182,7 +206,7 @@ def tile_bipartiteneuralmessagepassinglayer_pa_t_kernel(
             h_codes[n] = (codes, planes)
 
         def second_matmul(n):
-            acc2[n] = psum.tile([P, ED], F32, tag="s2", bufs=2, name="acc2_tile")
+            acc2[n] = psum.tile([P, ED], F32, tag="s2", bufs=1, name="acc2_tile")
             codes, planes = h_codes[n]
             nc.tensor.matmul_mx(
                 out=acc2[n][:],
@@ -198,8 +222,11 @@ def tile_bipartiteneuralmessagepassinglayer_pa_t_kernel(
             lat[n] = work.tile([P, ED], F32, tag="lat", bufs=6, name="lat_tile")
             nc.vector.tensor_tensor(out=lat[n][:], in0=acc2[n][:], in1=be2_all[:], op=ADD)
 
-        def finish(n):
-            nc.scalar.activation(out=lat[n][:], in_=lat[n][:], func=RELU)
+        def finish(n, vector=False):
+            if vector:
+                nc.vector.tensor_scalar(out=lat[n][:], in0=lat[n][:], scalar1=0.0, scalar2=None, op0=mybir.AluOpType.max)
+            else:
+                nc.scalar.activation(out=lat[n][:], in_=lat[n][:], func=RELU)
             nc.sync.dma_start(out=out_rows[n * P : (n + 1) * P, :], in_=lat[n][:])
 
         def sum_tile(n):
@@ -211,17 +238,21 @@ def tile_bipartiteneuralmessagepassinglayer_pa_t_kernel(
                 stop=(n == TILES - 1),
             )
 
-        ab_turned = psum.tile([P, 4, P], BF16, tag="xt", bufs=3, name="ab_turned")
-        widen(0)
-        nc.vector.tensor_copy(out=we_grouped[0][:, 0:2], in_=we_view(0, 0, 2))
-        turn(0)
-        for t in range(4):
-            nc.tensor.transpose(ab_turned[:, t, :], ab[:, t:ED:4], ident_bf[:])
-        nc.scalar.copy(out=we_grouped[0][:, 2:4], in_=we_view(0, 2, 4))
-        widen(1)
-        nc.scalar.copy(out=we_grouped[1][:, 2:4], in_=we_view(1, 2, 4))
+        ab_turned = psum.tile([P, 4, P], BF16, tag="xt", bufs=4, name="ab_turned")
         a_cols = keep.tile([P, NA, 4], F32, name="a_cols")
         b_cols = keep.tile([P, NB, 4], F32, name="b_cols")
+        widen(0, True)
+        widen(1)
+        turn(0)
+        we_group("s", 0, 2, 4)
+        turn(1)
+        for t in range(4):
+            nc.tensor.transpose(ab_turned[:, t, :], ab[:, t:ED:4], ident_bf[:])
+        widen(2)
+        product(0)
+        turn(2)
+        we_group("v", 0, 0, 2)
+        we_group("s", 1, 2, 4)
         nc.vector.tensor_tensor(
             out=a_cols[:],
             in0=ab_turned[:, :, 0:NA].rearrange("p t n -> p n t"),
@@ -229,15 +260,43 @@ def tile_bipartiteneuralmessagepassinglayer_pa_t_kernel(
             op=ADD,
         )
         nc.vector.tensor_copy(out=b_cols[:], in_=ab_turned[:, :, NA:P].rearrange("p t n -> p n t"))
-        turn(1)
+        make_addend(0)
+        make_addend(1)
+        product(1)
+        product(2)
+        widen(3)
+        we_group("v", 1, 0, 2)
+        we_quantize(0)
+        quantize_x(0)
+        we_quantize(1)
+        first_matmul(0)
+        turn(3)
+        quantize_x(1)
+        first_matmul(1)
+        quantize_x(2)
+        w2_group("s", ED // 2, ED)
+        w2_group("v", 0, ED // 2)
+        widen(4)
+        make_selectors(0, 2)
+        w2_quantize()
+        add_terms(0)
+        relu_hidden(0)
+        make_addend(2)
+        widen(5)
+        turn(4)
+        turn(5)
 
-        for n in range(TILES + 4):
+        load(6)
+        load(7)
+        load(8)
+
+        for n in range(3, TILES + 4):
             def live(m):
                 return 0 <= m < TILES
 
             if live(n - 1):
                 first_matmul(n - 1)
-            if live(n - 3):
+            if live(n - 3) and n > 3:
                 second_matmul(n - 3)
             if live(n - 4):
                 sum_tile(n - 4)
@@ -246,37 +305,27 @@ def tile_bipartiteneuralmessagepassinglayer_pa_t_kernel(
             if live(n - 2):
                 add_terms(n - 2)
                 relu_hidden(n - 2)
-            if live(n - 1):
-                make_addend(n - 1)
-            if live(n + 2):
-                widen(n + 2)
+            if live(n):
+                make_addend(n)
+            if live(n + 3):
+                widen(n + 3)
+            if n % 2 == 0 and n - 2 < TILES:
+                make_selectors(n - 2, n)
+            if n % 2 == 0 and live(n + 3):
                 turn(n + 2)
+                turn(n + 3)
             if live(n):
                 product(n)
-            if n == 0:
-                nc.vector.tensor_copy(out=we_grouped[1][:, 0:2], in_=we_view(1, 0, 2))
-                we_quantize(0)
+            if n == 3:
+                quantize_h(0)
+                second_matmul(0)
             if live(n - 3):
                 add_bias(n - 3)
-                finish(n - 3)
+                finish(n - 3, n - 3 == TILES - 1)
             if live(n):
                 quantize_x(n)
-            if n == 0:
-                we_quantize(1)
             if live(n - 2):
                 quantize_h(n - 2)
-            if n == 1:
-                nc.scalar.copy(
-                    out=w2_grouped[:, 0 : ED // 2], in_=w2_raw[:, :, 0 : ED // 2].rearrange("p j c -> p c j")
-                )
-                nc.vector.tensor_copy(
-                    out=w2_grouped[:, ED // 2 :], in_=w2_raw[:, :, ED // 2 :].rearrange("p j c -> p c j")
-                )
-                nc.vector.quantize_mx(
-                    out=w2_codes[:].bitcast(FP8X4),
-                    scales=w2_planes[:],
-                    in_=w2_grouped[:].rearrange("p c j -> p (c j)"),
-                )
 
         result = keep.tile([P, ED], F32, name="result")
         nc.vector.tensor_copy(out=result[:], in_=sums[:])

@@ -16,7 +16,6 @@ FP8X4 = mybir.dt.float8_e4m3fn_x4
 ADD = mybir.AluOpType.add
 MULT = mybir.AluOpType.mult
 AXIS_X = mybir.AxisListType.X
-COPY = mybir.ActivationFunctionType.Copy
 RELU = mybir.ActivationFunctionType.Relu
 
 P = 128
@@ -37,11 +36,12 @@ def tile_bipartiteneuralmessagepassinglayer_pa_t_kernel(
         psum = ctx.enter_context(tc.psum_pool(name="psum", bufs=1))
         ctx.enter_context(tc.manual_schedule())
 
+        scaled = {}
         byte_tiles, wide, turned, grouped, x_codes = {}, {}, {}, {}, {}
         addend, hidden, h_codes, acc1, acc2, lat = {}, {}, {}, {}, {}, {}
 
         def load(n):
-            tile_bytes = work.tile([P, K1], U8, tag="bytes", bufs=7, name="tile_bytes")
+            tile_bytes = work.tile([P, K1], U8, tag="bytes", bufs=10, name="tile_bytes")
             nc.sync.dma_start(out=tile_bytes[:], in_=x_rows[n * P : (n + 1) * P, :])
             byte_tiles[n] = tile_bytes
 
@@ -66,6 +66,8 @@ def tile_bipartiteneuralmessagepassinglayer_pa_t_kernel(
         nc.sync.dma_start(out=be2_all[:], in_=be2.partition_broadcast(P))
         load(4)
         load(5)
+        scale_row = keep.tile([P, 512], F32, name="scale_row")
+        nc.sync.dma_start(out=scale_row[:], in_=x_scale.rearrange("a b k -> (a b k)")[512:].partition_broadcast(P))
 
         ident = keep.tile([P, P], F32, name="ident")
         make_identity(nc, ident[:])
@@ -76,13 +78,16 @@ def tile_bipartiteneuralmessagepassinglayer_pa_t_kernel(
         nc.vector.tensor_reduce(out=halves[:], in_=ident[:].rearrange("p (h j) -> p h j", h=2), axis=AXIS_X, op=ADD)
         inner = keep.tile([P, NB], F32, name="inner")
         nc.vector.tensor_reduce(out=inner[:], in_=ident[:].rearrange("p (h j) -> p j h", h=2), axis=AXIS_X, op=ADD)
+        nc.vector.memset(sel[:, 0 * P : 16 * P].rearrange("p (n m) -> p n m", m=P)[:, :, NB:P], 0.0)
         sums = psum.tile([P, ED], F32, tag="sum", bufs=1, name="sums")
 
-        def make_selectors(lo, hi):
-            by_tile = sel[:, lo * P : hi * P].rearrange("p (n m) -> p n m", m=P)
-            wide_inner = inner[:].unsqueeze(1).to_broadcast([P, hi - lo, NB])
-            nc.scalar.copy(out=by_tile[:, :, 0:NB], in_=wide_inner)
-            nc.scalar.activation(out=by_tile[:, :, NB:P], in_=wide_inner, func=COPY, scale=0.0)
+        def make_inner(lo, hi):
+            nc.scalar.copy(
+                out=sel[:, lo * P : hi * P].rearrange("p (n m) -> p n m", m=P)[:, :, 0:NB],
+                in_=inner[:].unsqueeze(1).to_broadcast([P, hi - lo, NB]),
+            )
+
+        def make_outer(lo, hi):
             nc.scalar.copy(
                 out=sel[:, NB + lo * SEL_STEP : NB + hi * SEL_STEP].rearrange("p (n m) -> p n m", m=SEL_STEP)[:, :, 0:2],
                 in_=halves[:].unsqueeze(1).to_broadcast([P, hi - lo, 2]),
@@ -125,7 +130,7 @@ def tile_bipartiteneuralmessagepassinglayer_pa_t_kernel(
             )
 
         def widen(n, vector=False):
-            wide[n] = work.tile([P, K1], BF16, tag="wide", bufs=5, name="wide_tile")
+            wide[n] = work.tile([P, K1], BF16, tag="wide", bufs=8, name="wide_tile")
             if vector:
                 nc.vector.tensor_copy(out=wide[n][:], in_=byte_tiles[n][:].bitcast(FP8))
             else:
@@ -136,17 +141,42 @@ def tile_bipartiteneuralmessagepassinglayer_pa_t_kernel(
             words = wide[n][:].bitcast(F32)
             for g in range(2):
                 for u in range(2):
-                    nc.tensor.transpose(
-                        turned[n][:, g, :, u], words[:, 256 * g + u : 256 * (g + 1) : 2], ident[:]
-                    )
+                    source = words[:, 256 * g + u : 256 * (g + 1) : 2]
+                    if g == 1 and early(n):
+                        source = scaled[n][:, u].rearrange("p k e -> p (k e)").bitcast(F32)
+                    nc.tensor.transpose(turned[n][:, g, :, u], source, ident[:])
+
+        def early(n):
+            return n % 2 == 1 and n >= 11
+
+        def open_grouped(n):
+            grouped[n] = work.tile([P, 2, 512], BF16, tag="xg", bufs=4, align_bytes=64, name="grouped_tile")
+
+        def early_product(n, u):
+            if u == 0:
+                scaled[n] = work.tile([P, 2, P, 2], BF16, tag="scaled", bufs=2, name="scaled_tile")
+            nc.gpsimd.tensor_tensor(
+                out=scaled[n][:, u],
+                in0=wide[n][:, 512:].rearrange("p (k u e) -> p u k e", u=2, e=2)[:, u],
+                in1=scale_row[:].rearrange("p (k u e) -> p u k e", u=2, e=2)[:, u],
+                op=MULT,
+            )
+
+        def early_copy(n):
+            open_grouped(n)
+            nc.scalar.copy(
+                out=grouped[n][:, 1].bitcast(F32), in_=turned[n][:, 1].rearrange("p r u -> p (r u)")
+            )
 
         def product(n):
-            grouped[n] = work.tile([P, 2, 512], BF16, tag="xg", align_bytes=64, name="grouped_tile")
+            if not early(n):
+                open_grouped(n)
             values = turned[n][:].rearrange("p g r u -> p (g r u)").bitcast(BF16)
+            passes = 1 if early(n) else 2
             nc.vector.tensor_tensor(
-                out=grouped[n][:].rearrange("p g (r t) -> p g r t", t=4),
-                in0=values.rearrange("p (g r t) -> p g r t", g=2, t=4),
-                in1=scale[:].unsqueeze(2).to_broadcast([P, 2, P, 4]),
+                out=grouped[n][:, 0:passes].rearrange("p g (r t) -> p g r t", t=4),
+                in0=values.rearrange("p (g r t) -> p g r t", g=2, t=4)[:, 0:passes],
+                in1=scale[:, 0:passes].unsqueeze(2).to_broadcast([P, passes, P, 4]),
                 op=MULT,
             )
 
@@ -176,7 +206,7 @@ def tile_bipartiteneuralmessagepassinglayer_pa_t_kernel(
                     )
 
         def make_addend(n):
-            addend[n] = work.tile([P, 2, NB, 4], F32, tag="addend", bufs=2, name="addend_tile")
+            addend[n] = work.tile([P, 2, NB, 4], F32, tag="gate", bufs=3, align_bytes=64, name="addend_tile")
             for i in range(2):
                 nc.gpsimd.tensor_tensor(
                     out=addend[n][:, i],
@@ -195,7 +225,7 @@ def tile_bipartiteneuralmessagepassinglayer_pa_t_kernel(
             )
 
         def relu_hidden(n):
-            positive = work.tile([P, P * 4], BF16, tag="pos", align_bytes=64, name="positive_tile")
+            positive = work.tile([P, P * 4], BF16, tag="gate", bufs=3, align_bytes=64, name="positive_tile")
             nc.scalar.activation(out=positive[:], in_=hidden[n][:].rearrange("p e t -> p (e t)"), func=RELU)
             hidden[n] = positive
 
@@ -241,7 +271,9 @@ def tile_bipartiteneuralmessagepassinglayer_pa_t_kernel(
         ab_turned = psum.tile([P, 4, P], BF16, tag="xt", bufs=4, name="ab_turned")
         a_cols = keep.tile([P, NA, 4], F32, name="a_cols")
         b_cols = keep.tile([P, NB, 4], F32, name="b_cols")
+        make_inner(0, 16)
         widen(0, True)
+        nc.vector.memset(sel[:, 16 * P : TILES * P].rearrange("p (n m) -> p n m", m=P)[:, :, NB:P], 0.0)
         widen(1)
         turn(0)
         we_group("s", 0, 2, 4)
@@ -274,10 +306,10 @@ def tile_bipartiteneuralmessagepassinglayer_pa_t_kernel(
         quantize_x(1)
         first_matmul(1)
         quantize_x(2)
-        w2_group("s", ED // 2, ED)
-        w2_group("v", 0, ED // 2)
+        w2_group("s", 0, ED)
+        make_inner(16, TILES)
+        make_outer(0, TILES)
         widen(4)
-        make_selectors(0, 2)
         w2_quantize()
         add_terms(0)
         relu_hidden(0)
@@ -289,28 +321,35 @@ def tile_bipartiteneuralmessagepassinglayer_pa_t_kernel(
         load(6)
         load(7)
         load(8)
+        load(9)
+        load(10)
+        widened = 6
 
         for n in range(3, TILES + 4):
             def live(m):
                 return 0 <= m < TILES
 
-            if live(n - 1):
-                first_matmul(n - 1)
             if live(n - 3) and n > 3:
                 second_matmul(n - 3)
+            if live(n - 1):
+                first_matmul(n - 1)
             if live(n - 4):
                 sum_tile(n - 4)
-            if live(n + 6):
-                load(n + 6)
+            if 11 <= n + 8 < TILES:
+                load(n + 8)
             if live(n - 2):
                 add_terms(n - 2)
                 relu_hidden(n - 2)
-            if live(n):
+            if live(n) and n > 3:
                 make_addend(n)
-            if live(n + 3):
-                widen(n + 3)
-            if n % 2 == 0 and n - 2 < TILES:
-                make_selectors(n - 2, n)
+            ahead = n + 5 if n % 2 == 0 else n + 4
+            if live(ahead) and early(ahead):
+                early_product(ahead, n % 2)
+            while widened < TILES and widened <= n + 3 + min(3, n - 2):
+                widen(widened)
+                widened += 1
+            if live(n + 1) and early(n + 1):
+                early_copy(n + 1)
             if n % 2 == 0 and live(n + 3):
                 turn(n + 2)
                 turn(n + 3)
@@ -318,11 +357,14 @@ def tile_bipartiteneuralmessagepassinglayer_pa_t_kernel(
                 product(n)
             if n == 3:
                 quantize_h(0)
+                make_addend(3)
                 second_matmul(0)
+            if n == 3:
+                quantize_x(n)
             if live(n - 3):
                 add_bias(n - 3)
                 finish(n - 3, n - 3 == TILES - 1)
-            if live(n):
+            if live(n) and n > 3:
                 quantize_x(n)
             if live(n - 2):
                 quantize_h(n - 2)

from contextlib import ExitStack

import concourse.mybir as mybir
from concourse.masks import make_identity

NA, NB, K1, ED = 64, 64, 1024, 512
E = NA * NB
FLOPS = 2 * E * (K1 * ED + ED * ED)

F32 = mybir.dt.float32
BF16 = mybir.dt.bfloat16
U32 = mybir.dt.uint32
U8 = mybir.dt.uint8
FP8 = mybir.dt.float8_e4m3fn
FP8X4 = mybir.dt.float8_e4m3fn_x4
ADD = mybir.AluOpType.add
MULT = mybir.AluOpType.mult
AXIS_X = mybir.AxisListType.X
RELU = mybir.ActivationFunctionType.Relu

P = 128
TILES = E // P
SEL_STEP = P + 2


def tile_bipartiteneuralmessagepassinglayer_pa_t_kernel(
    tc, x_bytes, x_scale, a_proj, b_proj, we, be1, we2, be2, out_edge, out_a, out_b
):
    nc = tc.nc
    x_rows = x_bytes.rearrange("i j k -> (i j) k")
    out_rows = out_edge.rearrange("i j c -> (i j) c")

    with ExitStack() as ctx:
        keep = ctx.enter_context(tc.tile_pool(name="keep", bufs=1))
        work = ctx.enter_context(tc.tile_pool(name="work", bufs=3))
        psum = ctx.enter_context(tc.psum_pool(name="psum", bufs=1))
        ctx.enter_context(tc.manual_schedule())

        scaled = {}
        byte_tiles, wide, turned, grouped, x_codes = {}, {}, {}, {}, {}
        addend, hidden, h_codes, acc1, acc2, lat = {}, {}, {}, {}, {}, {}

        def load(n):
            tile_bytes = work.tile([P, K1], U8, tag="bytes", bufs=10, name="tile_bytes")
            nc.sync.dma_start(out=tile_bytes[:], in_=x_rows[n * P : (n + 1) * P, :])
            byte_tiles[n] = tile_bytes

        load(0)
        scale = keep.tile([P, 2, 4], F32, name="scale")
        nc.scalar.dma_start(out=scale[:], in_=x_scale.rearrange("a b (g p t) -> p (a b g) t", p=P, t=4))
        ab = keep.tile([P, ED], BF16, name="ab")
        nc.scalar.dma_start(out=ab[0:NA, :], in_=a_proj)
        nc.scalar.dma_start(out=ab[NA:P, :], in_=b_proj)
        be1_col = keep.tile([P, 4], BF16, name="be1_col")
        nc.scalar.dma_start(out=be1_col[:], in_=be1.rearrange("(p t) -> p t", t=4))
        we_raw = []
        for g in range(2):
            raw = keep.tile([P, 4, ED], BF16, name="we_raw%d" % g)
            nc.sync.dma_start(out=raw[:], in_=we[g * 512 : (g + 1) * 512, :].rearrange("(p j) c -> p j c", j=4))
            we_raw.append(raw)
            load(1 + g)
        load(3)
        w2_raw = keep.tile([P, 4, ED], BF16, name="w2_raw")
        nc.sync.dma_start(out=w2_raw[:], in_=we2.rearrange("(p j) c -> p j c", j=4))
        be2_all = keep.tile([P, ED], BF16, name="be2_all")
        nc.sync.dma_start(out=be2_all[:], in_=be2.partition_broadcast(P))
        load(4)
        load(5)
        scale_row = keep.tile([P, 512], F32, name="scale_row")
        nc.sync.dma_start(out=scale_row[:], in_=x_scale.rearrange("a b k -> (a b k)")[512:].partition_broadcast(P))

        ident = keep.tile([P, P], F32, name="ident")
        make_identity(nc, ident[:])
        ident_bf = keep.tile([P, P], BF16, name="ident_bf")
        nc.vector.tensor_copy(out=ident_bf[:], in_=ident[:])
        sel = keep.tile([P, NB + TILES * SEL_STEP], F32, name="sel")
        halves = keep.tile([P, 2], F32, name="halves")
        nc.vector.tensor_reduce(out=halves[:], in_=ident[:].rearrange("p (h j) -> p h j", h=2), axis=AXIS_X, op=ADD)
        inner = keep.tile([P, NB], F32, name="inner")
        nc.vector.tensor_reduce(out=inner[:], in_=ident[:].rearrange("p (h j) -> p j h", h=2), axis=AXIS_X, op=ADD)
        nc.vector.memset(sel[:, 0 * P : 16 * P].rearrange("p (n m) -> p n m", m=P)[:, :, NB:P], 0.0)
        sums = psum.tile([P, ED], F32, tag="sum", bufs=1, name="sums")

        def make_inner(lo, hi):
            nc.scalar.copy(
                out=sel[:, lo * P : hi * P].rearrange("p (n m) -> p n m", m=P)[:, :, 0:NB],
                in_=inner[:].unsqueeze(1).to_broadcast([P, hi - lo, NB]),
            )

        def make_outer(lo, hi):
            nc.scalar.copy(
                out=sel[:, NB + lo * SEL_STEP : NB + hi * SEL_STEP].rearrange("p (n m) -> p n m", m=SEL_STEP)[:, :, 0:2],
                in_=halves[:].unsqueeze(1).to_broadcast([P, hi - lo, 2]),
            )

        we_codes = keep.tile([P, 2, ED], U32, align_bytes=64, name="we_codes")
        we_planes = keep.tile([P, 2, ED], U8, align_bytes=64, name="we_planes")
        w2_codes = keep.tile([P, ED], U32, align_bytes=64, name="w2_codes")
        w2_planes = keep.tile([P, ED], U8, align_bytes=64, name="w2_planes")
        we_grouped = [keep.tile([P, 4, P, 4], BF16, align_bytes=64, name="we_grouped%d" % g) for g in range(2)]
        w2_grouped = keep.tile([P, ED, 4], BF16, align_bytes=64, name="w2_grouped")

        def we_view(g, lo, hi):
            return we_raw[g][:].rearrange("p j (m t) -> p t m j", t=4)[:, lo:hi]

        def regroup(engine, out, in_):
            if engine == "g":
                nc.gpsimd.tensor_scalar(out=out, in0=in_, scalar1=1.0, scalar2=0.0, op0=MULT, op1=ADD)
            elif engine == "s":
                nc.scalar.copy(out=out, in_=in_)
            else:
                nc.vector.tensor_copy(out=out, in_=in_)

        def we_group(engine, g, lo, hi):
            regroup(engine, we_grouped[g][:, lo:hi], we_view(g, lo, hi))

        def w2_group(engine, lo, hi):
            regroup(engine, w2_grouped[:, lo:hi], w2_raw[:, :, lo:hi].rearrange("p j c -> p c j"))

        def w2_quantize():
            nc.vector.quantize_mx(
                out=w2_codes[:].bitcast(FP8X4), scales=w2_planes[:], in_=w2_grouped[:].rearrange("p c j -> p (c j)")
            )

        def we_quantize(g):
            nc.vector.quantize_mx(
                out=we_codes[:, g, :].bitcast(FP8X4),
                scales=we_planes[:, g, :],
                in_=we_grouped[g][:].rearrange("p t m j -> p (t m j)"),
            )

        def widen(n, vector=False):
            wide[n] = work.tile([P, K1], BF16, tag="wide", bufs=8, name="wide_tile")
            if vector:
                nc.vector.tensor_copy(out=wide[n][:], in_=byte_tiles[n][:].bitcast(FP8))
            else:
                nc.scalar.copy(out=wide[n][:], in_=byte_tiles[n][:].bitcast(FP8))

        def turn(n):
            turned[n] = psum.tile([P, 2, P, 2], F32, tag="xt", bufs=4, name="turned_tile")
            words = wide[n][:].bitcast(F32)
            for g in range(2):
                for u in range(2):
                    source = words[:, 256 * g + u : 256 * (g + 1) : 2]
                    if g == 1 and early(n):
                        source = scaled[n][:, u].rearrange("p k e -> p (k e)").bitcast(F32)
                    nc.tensor.transpose(turned[n][:, g, :, u], source, ident[:])

        def early(n):
            return n % 2 == 1 and n >= 11

        def open_grouped(n):
            grouped[n] = work.tile([P, 2, 512], BF16, tag="xg", bufs=4, align_bytes=64, name="grouped_tile")

        def early_product(n, u):
            if u == 0:
                scaled[n] = work.tile([P, 2, P, 2], BF16, tag="scaled", bufs=2, name="scaled_tile")
            nc.gpsimd.tensor_tensor(
                out=scaled[n][:, u],
                in0=wide[n][:, 512:].rearrange("p (k u e) -> p u k e", u=2, e=2)[:, u],
                in1=scale_row[:].rearrange("p (k u e) -> p u k e", u=2, e=2)[:, u],
                op=MULT,
            )

        def early_copy(n):
            open_grouped(n)
            nc.scalar.copy(
                out=grouped[n][:, 1].bitcast(F32), in_=turned[n][:, 1].rearrange("p r u -> p (r u)")
            )

        def product(n):
            if not early(n):
                open_grouped(n)
            values = turned[n][:].rearrange("p g r u -> p (g r u)").bitcast(BF16)
            passes = 1 if early(n) else 2
            nc.vector.tensor_tensor(
                out=grouped[n][:, 0:passes].rearrange("p g (r t) -> p g r t", t=4),
                in0=values.rearrange("p (g r t) -> p g r t", g=2, t=4)[:, 0:passes],
                in1=scale[:, 0:passes].unsqueeze(2).to_broadcast([P, passes, P, 4]),
                op=MULT,
            )

        def quantize_x(n):
            codes = work.tile([P, 2, P], U32, tag="xq", align_bytes=64, name="x_code_tile")
            planes = work.tile([P, 2, P], U8, tag="xs", align_bytes=64, name="x_plane_tile")
            nc.vector.quantize_mx(
                out=codes[:].rearrange("p g r -> p (g r)").bitcast(FP8X4),
                scales=planes[:].rearrange("p g r -> p (g r)"),
                in_=grouped[n][:].rearrange("p g w -> p (g w)"),
            )
            x_codes[n] = (codes, planes)

        def first_matmul(n):
            acc1[n] = psum.tile([P, 4, P], F32, tag="s1", bufs=2, name="acc1_tile")
            codes, planes = x_codes[n]
            for t in range(4):
                for g in range(2):
                    nc.tensor.matmul_mx(
                        out=acc1[n][:, t, :],
                        lhsT=we_codes[:, g, t * P : (t + 1) * P].bitcast(FP8X4),
                        lhsT_scale=we_planes[:, g, t * P : (t + 1) * P],
                        rhs=codes[:, g, :].bitcast(FP8X4),
                        rhs_scale=planes[:, g, :],
                        start=(g == 0),
                        stop=(g == 1),
                    )

        def make_addend(n):
            addend[n] = work.tile([P, 2, NB, 4], F32, tag="gate", bufs=3, align_bytes=64, name="addend_tile")
            for i in range(2):
                nc.gpsimd.tensor_tensor(
                    out=addend[n][:, i],
                    in0=b_cols[:],
                    in1=a_cols[:, 2 * n + i, :].unsqueeze(1).to_broadcast([P, NB, 4]),
                    op=ADD,
                )

        def add_terms(n):
            hidden[n] = work.tile([P, P, 4], BF16, tag="hid", align_bytes=64, name="hidden_tile")
            nc.vector.tensor_tensor(
                out=hidden[n][:],
                in0=acc1[n][:].rearrange("p t e -> p e t"),
                in1=addend[n][:].rearrange("p i j t -> p (i j) t"),
                op=ADD,
            )

        def relu_hidden(n):
            positive = work.tile([P, P * 4], BF16, tag="gate", bufs=3, align_bytes=64, name="positive_tile")
            nc.scalar.activation(out=positive[:], in_=hidden[n][:].rearrange("p e t -> p (e t)"), func=RELU)
            hidden[n] = positive

        def quantize_h(n):
            codes = work.tile([P, P], U32, tag="hq", align_bytes=64, name="h_code_tile")
            planes = work.tile([P, P], U8, tag="hs", align_bytes=64, name="h_plane_tile")
            nc.vector.quantize_mx(out=codes[:].bitcast(FP8X4), scales=planes[:], in_=hidden[n][:])
            h_codes[n] = (codes, planes)

        def second_matmul(n):
            acc2[n] = psum.tile([P, ED], F32, tag="s2", bufs=1, name="acc2_tile")
            codes, planes = h_codes[n]
            nc.tensor.matmul_mx(
                out=acc2[n][:],
                lhsT=codes[:].bitcast(FP8X4),
                lhsT_scale=planes[:],
                rhs=w2_codes[:].bitcast(FP8X4),
                rhs_scale=w2_planes[:],
                start=True,
                stop=True,
            )

        def add_bias(n):
            lat[n] = work.tile([P, ED], F32, tag="lat", bufs=6, name="lat_tile")
            nc.vector.tensor_tensor(out=lat[n][:], in0=acc2[n][:], in1=be2_all[:], op=ADD)

        def finish(n, vector=False):
            if vector:
                nc.vector.tensor_scalar(out=lat[n][:], in0=lat[n][:], scalar1=0.0, scalar2=None, op0=mybir.AluOpType.max)
            else:
                nc.scalar.activation(out=lat[n][:], in_=lat[n][:], func=RELU)
            nc.sync.dma_start(out=out_rows[n * P : (n + 1) * P, :], in_=lat[n][:])

        def sum_tile(n):
            nc.tensor.matmul(
                out=sums[:],
                lhsT=sel[:, n * P : (n + 1) * P],
                rhs=lat[n][:],
                start=(n == 0),
                stop=(n == TILES - 1),
            )

        ab_turned = psum.tile([P, 4, P], BF16, tag="xt", bufs=4, name="ab_turned")
        a_cols = keep.tile([P, NA, 4], F32, name="a_cols")
        b_cols = keep.tile([P, NB, 4], F32, name="b_cols")
        make_inner(0, 16)
        widen(0, True)
        nc.vector.memset(sel[:, 16 * P : TILES * P].rearrange("p (n m) -> p n m", m=P)[:, :, NB:P], 0.0)
        widen(1)
        turn(0)
        we_group("s", 0, 2, 4)
        turn(1)
        for t in range(4):
            nc.tensor.transpose(ab_turned[:, t, :], ab[:, t:ED:4], ident_bf[:])
        widen(2)
        product(0)
        turn(2)
        we_group("v", 0, 0, 2)
        we_group("s", 1, 2, 4)
        nc.vector.tensor_tensor(
            out=a_cols[:],
            in0=ab_turned[:, :, 0:NA].rearrange("p t n -> p n t"),
            in1=be1_col[:].unsqueeze(1).to_broadcast([P, NA, 4]),
            op=ADD,
        )
        nc.vector.tensor_copy(out=b_cols[:], in_=ab_turned[:, :, NA:P].rearrange("p t n -> p n t"))
        make_addend(0)
        make_addend(1)
        product(1)
        product(2)
        widen(3)
        we_group("v", 1, 0, 2)
        we_quantize(0)
        quantize_x(0)
        we_quantize(1)
        first_matmul(0)
        turn(3)
        quantize_x(1)
        first_matmul(1)
        quantize_x(2)
        w2_group("s", 0, ED)
        make_inner(16, TILES)
        make_outer(0, TILES)
        widen(4)
        w2_quantize()
        add_terms(0)
        relu_hidden(0)
        make_addend(2)
        widen(5)
        turn(4)
        turn(5)

        load(6)
        load(7)
        load(8)
        load(9)
        load(10)
        widened = 6

        for n in range(3, TILES + 4):
            def live(m):
                return 0 <= m < TILES

            if live(n - 3) and n > 3:
                second_matmul(n - 3)
            if live(n - 1):
                first_matmul(n - 1)
            if live(n - 4):
                sum_tile(n - 4)
            if 11 <= n + 8 < TILES:
                load(n + 8)
            if live(n - 2):
                add_terms(n - 2)
                relu_hidden(n - 2)
            if live(n) and n > 3:
                make_addend(n)
            ahead = n + 5 if n % 2 == 0 else n + 4
            if live(ahead) and early(ahead):
                early_product(ahead, n % 2)
            while widened < TILES and widened <= n + 3 + min(3, n - 2):
                widen(widened)
                widened += 1
            if live(n + 1) and early(n + 1):
                early_copy(n + 1)
            if n % 2 == 0 and live(n + 3):
                turn(n + 2)
                turn(n + 3)
            if live(n):
                product(n)
            if n == 3:
                quantize_h(0)
                make_addend(3)
                second_matmul(0)
            if n == 3:
                quantize_x(n)
            if live(n - 3):
                add_bias(n - 3)
                finish(n - 3, n - 3 == TILES - 1)
            if live(n) and n > 3:
                quantize_x(n)
            if live(n - 2):
                quantize_h(n - 2)

        result = keep.tile([P, ED], F32, name="result")
        nc.vector.tensor_copy(out=result[:], in_=sums[:])
        nc.sync.dma_start(out=out_b, in_=result[0:NB, :])
        nc.sync.dma_start(out=out_a, in_=result[NB:P, :])
